import numpy as np
import ml_dtypes


def mxq(x, axis, fmt="e4m3"):
    dtype, down = {"e4m3": (ml_dtypes.float8_e4m3fn, 7), "e5m2": (ml_dtypes.float8_e5m2, 14)}[fmt]
    v = np.moveaxis(np.asarray(x, np.float32).astype(ml_dtypes.bfloat16).astype(np.float64), axis, -1)
    blocks = v.reshape(v.shape[:-1] + (-1, 32))
    amax = np.abs(blocks).max(-1, keepdims=True)
    byte = np.maximum(np.where(amax > 0, np.frexp(amax)[1] - 1 + 127, 0) - down, 1)
    scale = np.exp2(byte - 127.0)
    codes = (blocks / scale).astype(np.float32).astype(dtype).astype(np.float64)
    return np.moveaxis((codes * scale).reshape(v.shape), -1, axis)


WIDE = False


def mx_kscale(k):
    if not WIDE:
        return np.ones(k)
    levels = np.array([10, -10, 5, -5, 0])
    a = np.random.permutation(np.resize(levels, k // 512 * 4)).reshape(k // 512, 4)
    idx = np.arange(k)
    return np.exp2(a[idx // 512, idx % 128 // 32])


BF16 = ml_dtypes.bfloat16


def bf(x):
    return np.asarray(x, np.float32).astype(BF16)


def f64(x):
    return np.asarray(x).astype(np.float64)


E2M1 = np.array([0.0, 0.5, 1.0, 1.5, 2.0, 3.0, 4.0, 6.0, -0.0, -0.5, -1.0, -1.5, -2.0, -3.0, -4.0, -6.0])


def pack_weight(w, fmt):
    k, n = w.shape
    w = f64(bf(w)).reshape(k // 32, 32, n)
    amax = np.abs(w).max(1)
    if fmt == "e4m3":
        byte = np.frexp(amax)[1] - 1 + 127 - 7
    else:
        mant, ex = np.frexp(amax / 6.0)
        byte = np.where(mant > 0.5, ex, ex - 1) + 127
    byte = np.clip(np.where(amax > 0, byte, 1), 1, 254)
    scaled = (w * np.exp2(127.0 - byte)[:, None, :]).reshape(k, n).astype(np.float32)
    by_word = np.ascontiguousarray(scaled.reshape(k // 512, 128, 4, n).transpose(0, 1, 3, 2))
    if fmt == "e4m3":
        words = by_word.astype(ml_dtypes.float8_e4m3fn).view(np.uint8)
    else:
        c = by_word.astype(ml_dtypes.float4_e2m1fn).view(np.uint8) & 0xF
        words = c[..., 0::2] | (c[..., 1::2] << 4)
    return np.ascontiguousarray(words), np.ascontiguousarray(byte.astype(np.uint8).reshape(k // 512, 16, n))


def unpack_weight(words, scales, fmt):
    g, p, n, _ = words.shape
    if fmt == "e4m3":
        vals = np.ascontiguousarray(words).view(ml_dtypes.float8_e4m3fn).astype(np.float64)
    else:
        nib = np.empty((g, p, n, 4), np.uint8)
        nib[..., 0::2] = words & 0xF
        nib[..., 1::2] = words >> 4
        vals = E2M1[nib]
    vals = vals * np.repeat(np.exp2(scales.astype(np.float64) - 127.0), 8, axis=1)[..., None]
    return vals.transpose(0, 1, 3, 2).reshape(g * 512, n)


M, K, N = 2048, 1024, 512
EPS = 1e-05


def setup_inputs():
    s = mx_kscale(K)
    x = bf(np.random.standard_normal((M, K)) * s)
    weight = np.random.standard_normal((N, K)) / np.sqrt(K) / s[None, :]
    weight_words, weight_scales = pack_weight(np.ascontiguousarray(weight.T), "e4m3")
    return {"x": x,
            "weight_words": weight_words,
            "weight_scales": weight_scales,
            "bias": bf(np.random.standard_normal(N) * 0.5),
            "gamma": bf(1.0 + 0.1 * np.random.standard_normal(N)),
            "beta": bf(0.1 * np.random.standard_normal(N)),
            "scale": bf(2.0 + 0.1 * np.random.standard_normal(1))}


def reference(x, weight_words, weight_scales, bias, gamma, beta, scale):
    acc = (mxq(f64(x), 1, "e4m3") @ unpack_weight(weight_words, weight_scales, "e4m3")) + f64(bias)[None, :]
    mean = np.mean(acc, axis=1, keepdims=True)
    var = np.mean((acc - mean) ** 2, axis=1, keepdims=True)
    normalized = (acc - mean) / np.sqrt(var + EPS)
    scaled = (normalized * f64(gamma)[None, :] + f64(beta)[None, :]) * f64(scale)[0]
    e = np.exp(scaled - scaled.max(axis=1, keepdims=True))
    return e / e.sum(axis=1, keepdims=True)

@@ -1,0 +1,243 @@
+from contextlib import ExitStack
+
+import concourse.mybir as mybir
+from concourse.masks import make_identity
+
+F32 = mybir.dt.float32
+BF16 = mybir.dt.bfloat16
+I32 = mybir.dt.int32
+U32 = mybir.dt.uint32
+U8 = mybir.dt.uint8
+FP8X4 = mybir.dt.float8_e4m3fn_x4
+ALU = mybir.AluOpType
+ACT = mybir.ActivationFunctionType
+AXIS = mybir.AxisListType
+
+M, K, N = 2048, 1024, 512
+EPS = 1e-05
+FLOPS = 2 * M * K * N
+
+P = 128
+PACK = 4
+K_PASS = P * PACK
+PASSES = K // K_PASS
+HALVES = 2
+ROW_TILES = M // P
+PAIR = 2
+PAIRS = ROW_TILES // PAIR
+
+
+def tile_modelnew_kernel(tc, x, weight_words, weight_scales, bias, gamma, beta, scale, out):
+    nc = tc.nc
+    with ExitStack() as ctx:
+        const = ctx.enter_context(tc.tile_pool(name="const", bufs=1))
+        xin = ctx.enter_context(tc.tile_pool(name="xin", bufs=ROW_TILES))
+        quant = ctx.enter_context(tc.tile_pool(name="quant", bufs=3))
+        work = ctx.enter_context(tc.tile_pool(name="work", bufs=6))
+        stats = ctx.enter_context(tc.tile_pool(name="stats", bufs=4))
+        psum_const = ctx.enter_context(tc.psum_pool(name="psum_const", bufs=1))
+        psum_xt = ctx.enter_context(tc.psum_pool(name="psum_xt", bufs=2))
+        psum_acc = ctx.enter_context(tc.psum_pool(name="psum_acc", bufs=4))
+
+        w_scales = const.tile([P, PASSES, N], U8, align_bytes=64)
+        nc.vector.memset(w_scales[:].bitcast(I32), 0)
+        vec_rows = const.tile([P, 3, N], BF16)
+        nc.vector.memset(vec_rows[:], 0.0)
+        ones = const.tile([P, P], BF16)
+        nc.vector.memset(ones[:], 1.0)
+        neg_half = const.tile([P, PAIR], F32)
+        nc.vector.memset(neg_half[:], -0.5)
+        ident = const.tile([P, P], F32)
+        make_identity(nc, ident[:])
+        table_warm = const.tile([P, 1], F32)
+        nc.scalar.activation(out=table_warm[:], in_=neg_half[:, 0:1], func=ACT.Exp)
+
+        x_tiles = []
+        for i in range(ROW_TILES):
+            x_tile = xin.tile([P, K], BF16, name="x_tile")
+            x_tiles.append(x_tile)
+
+        def load_x(i):
+            nc.sync.dma_start(out=x_tiles[i][:], in_=x[i * P : (i + 1) * P, :])
+
+        for i in range(PAIR):
+            load_x(i)
+        for quadrant in range(4):
+            nc.sync.dma_start(
+                out=w_scales[32 * quadrant : 32 * quadrant + 4, :, :].bitcast(I32),
+                in_=weight_scales[:, 4 * quadrant : 4 * quadrant + 4, :].rearrange("g r n -> r g n").bitcast(I32),
+            )
+        w_codes = const.tile([P, PASSES, PACK * N], U8, align_bytes=64)
+        nc.sync.dma_start(
+            out=w_codes[:].bitcast(I32),
+            in_=weight_words.rearrange("g p n t -> p g (n t)").bitcast(I32),
+        )
+        for i in range(PAIR, ROW_TILES):
+            load_x(i)
+
+        scale_col = const.tile([P, 1], BF16)
+        nc.scalar.dma_start(out=scale_col[:], in_=scale.partition_broadcast(P))
+        nc.scalar.dma_start(out=vec_rows[0:1, 0, :], in_=bias.unsqueeze(0))
+        nc.scalar.dma_start(out=vec_rows[0:1, 1, :], in_=gamma.unsqueeze(0))
+        nc.scalar.dma_start(out=vec_rows[0:1, 2, :], in_=beta.unsqueeze(0))
+
+        bias_ps = psum_acc.tile([P, N], F32, name="acc")
+        nc.tensor.matmul(out=bias_ps[:], lhsT=ones[:], rhs=vec_rows[:, 0, :], start=True, stop=True)
+        bias_all = const.tile([P, N], F32)
+        nc.scalar.copy(out=bias_all[:], in_=bias_ps[:])
+        gain = psum_const.tile([P, N], F32)
+        nc.tensor.matmul(
+            out=gain[:], lhsT=scale_col[:, 0:1].to_broadcast([P, P]), rhs=vec_rows[:, 1, :], start=True, stop=True
+        )
+        shift = psum_const.tile([P, N], F32)
+        nc.tensor.matmul(
+            out=shift[:], lhsT=scale_col[:, 0:1].to_broadcast([P, P]), rhs=vec_rows[:, 2, :], start=True, stop=True
+        )
+
+        xts, groupeds, codes, accs, ts, centreds, zs, es = {}, {}, {}, {}, {}, {}, {}, {}
+        neg_means, rstds, neg_maxs, exp_sums, inv_sums = {}, {}, {}, {}, {}
+
+        def transpose_x(pair):
+            xts[pair] = []
+            for j in range(PAIR):
+                x_words = x_tiles[pair * PAIR + j][:].bitcast(F32)
+                xt = psum_xt.tile([P, PASSES, HALVES, P], F32, name="xt")
+                for g in range(PASSES):
+                    for u in range(HALVES):
+                        nc.tensor.transpose(
+                            xt[:, g, u, :],
+                            x_words[:, (K_PASS // 2) * g + u : (K_PASS // 2) * (g + 1) : HALVES],
+                            ident[:],
+                        )
+                xts[pair].append(xt)
+
+        def regroup_x(pair):
+            grouped = quant.tile([P, PAIR, PASSES, P, PACK], BF16, align_bytes=64, name="grouped")
+            for j in range(PAIR):
+                nc.scalar.copy(
+                    out=grouped[:, j].bitcast(F32),
+                    in_=xts[pair][j][:].rearrange("p g u r -> p g r u"),
+                )
+            groupeds[pair] = grouped
+
+        def quantise_x(pair):
+            x_codes = quant.tile([P, PAIR, PASSES, P], U32, align_bytes=64, name="x_codes")
+            x_scales = quant.tile([P, PAIR, PASSES, P], U8, align_bytes=64, name="x_scales")
+            nc.vector.quantize_mx(
+                out=x_codes[:].rearrange("p j g r -> p (j g r)").bitcast(FP8X4),
+                scales=x_scales[:].rearrange("p j g r -> p (j g r)"),
+                in_=groupeds[pair][:].rearrange("p j g r t -> p (j g r t)"),
+            )
+            codes[pair] = (x_codes, x_scales)
+
+        def multiply(pair):
+            x_codes, x_scales = codes[pair]
+            accs[pair] = []
+            for j in range(PAIR):
+                acc = psum_acc.tile([P, N], F32, name="acc")
+                for g in range(PASSES):
+                    nc.tensor.matmul_mx(
+                        out=acc[:],
+                        lhsT=x_codes[:, j, g, :].bitcast(FP8X4),
+                        lhsT_scale=x_scales[:, j, g, :],
+                        rhs=w_codes[:, g, :].bitcast(FP8X4),
+                        rhs_scale=w_scales[:, g, :],
+                        start=(g == 0),
+                        stop=(g == PASSES - 1),
+                    )
+                accs[pair].append(acc)
+
+        def add_bias(pair):
+            row_sum = stats.tile([P, PAIR], F32, name="row_sum")
+            ts[pair] = []
+            for j in range(PAIR):
+                t = work.tile([P, N], F32, name="t")
+                nc.vector.scalar_tensor_tensor(
+                    out=t[:], in0=accs[pair][j][:], scalar=1.0, in1=bias_all[:], op0=ALU.mult, op1=ALU.add,
+                    accum_out=row_sum[:, j : j + 1],
+                )
+                ts[pair].append(t)
+            neg_mean = stats.tile([P, PAIR], F32, name="neg_mean")
+            nc.vector.tensor_scalar(out=neg_mean[:], in0=row_sum[:], scalar1=-1.0 / N, scalar2=None, op0=ALU.mult)
+            neg_means[pair] = neg_mean
+
+        def variance(pair):
+            sq_sum = stats.tile([P, PAIR], F32, name="sq_sum")
+            for j in range(PAIR):
+                squares = work.tile([P, N], F32, name="squares")
+                nc.scalar.activation(
+                    out=squares[:], in_=ts[pair][j][:], func=ACT.Square, bias=neg_means[pair][:, j : j + 1],
+                    scale=1.0, accum_out=sq_sum[:, j : j + 1],
+                )
+            var_eps = stats.tile([P, PAIR], F32, name="var_eps")
+            nc.gpsimd.tensor_scalar(
+                out=var_eps[:], in0=sq_sum[:], scalar1=1.0 / N, scalar2=EPS, op0=ALU.mult, op1=ALU.add
+            )
+            rstd = stats.tile([P, PAIR], F32, name="rstd")
+            nc.gpsimd.tensor_tensor(out=rstd[:], in0=var_eps[:], in1=neg_half[:], op=ALU.pow)
+            rstds[pair] = rstd
+
+        def centre_and_gain(pair):
+            centreds[pair] = []
+            for j in range(PAIR):
+                centred = work.tile([P, N], F32, name="centred")
+                nc.vector.scalar_tensor_tensor(
+                    out=centred[:], in0=ts[pair][j][:], scalar=neg_means[pair][:, j : j + 1], in1=gain[:],
+                    op0=ALU.add, op1=ALU.mult,
+                )
+                centreds[pair].append(centred)
+
+        def normalise_and_max(pair):
+            neg_max = stats.tile([P, PAIR], F32, name="neg_max")
+            zs[pair] = []
+            for j in range(PAIR):
+                z = work.tile([P, N], F32, name="z")
+                nc.vector.scalar_tensor_tensor(
+                    out=z[:], in0=centreds[pair][j][:], scalar=rstds[pair][:, j : j + 1], in1=shift[:],
+                    op0=ALU.mult, op1=ALU.add,
+                )
+                nc.vector.tensor_reduce(out=neg_max[:, j : j + 1], in_=z[:], axis=AXIS.X, op=ALU.max, negate=True)
+                zs[pair].append(z)
+            neg_maxs[pair] = neg_max
+
+        def exponentials(pair):
+            exp_sum = stats.tile([P, PAIR], F32, name="exp_sum")
+            es[pair] = []
+            for j in range(PAIR):
+                e = work.tile([P, N], F32, name="e")
+                nc.scalar.activation(
+                    out=e[:], in_=zs[pair][j][:], func=ACT.Exp, bias=neg_maxs[pair][:, j : j + 1], scale=1.0,
+                    accum_out=exp_sum[:, j : j + 1],
+                )
+                es[pair].append(e)
+            exp_sums[pair] = exp_sum
+
+        def invert_sums(pair):
+            inv_sum = stats.tile([P, PAIR], F32, name="inv_sum")
+            nc.vector.reciprocal(out=inv_sum[:], in_=exp_sums[pair][:])
+            inv_sums[pair] = inv_sum
+
+        def divide_and_store(pair):
+            for j in range(PAIR):
+                row0 = (pair * PAIR + j) * P
+                probs = work.tile([P, N], F32, name="probs")
+                nc.scalar.activation(out=probs[:], in_=es[pair][j][:], func=ACT.Copy, scale=inv_sums[pair][:, j : j + 1])
+                nc.sync.dma_start(out=out[row0 : row0 + P, :], in_=probs[:])
+
+        def run(stage, pair):
+            if 0 <= pair < PAIRS:
+                stage(pair)
+
+        with tc.manual_schedule():
+            for step in range(-3, PAIRS + 2):
+                run(quantise_x, step + 1)
+                run(multiply, step + 1)
+                run(divide_and_store, step - 2)
+                run(regroup_x, step + 2)
+                run(add_bias, step)
+                run(variance, step)
+                run(normalise_and_max, step - 1)
+                run(exponentials, step - 1)
+                run(centre_and_gain, step)
+                run(invert_sums, step - 1)
+                run(transpose_x, step + 3)

@@ -95,7 +95,7 @@ def tile_modelnew_kernel(tc, x, weight_words, weight_scales, bias, gamma, beta, 
         )
 
         xts, groupeds, codes, accs, ts, centreds, zs, es = {}, {}, {}, {}, {}, {}, {}, {}
-        neg_means, rstds, neg_maxs, exp_sums, inv_sums = {}, {}, {}, {}, {}
+        row_sums, neg_means, rstds, neg_maxs, exp_sums, inv_sums = {}, {}, {}, {}, {}, {}
 
         def transpose_x(pair):
             xts[pair] = []
@@ -123,11 +123,12 @@ def tile_modelnew_kernel(tc, x, weight_words, weight_scales, bias, gamma, beta, 
         def quantise_x(pair):
             x_codes = quant.tile([P, PAIR, PASSES, P], U32, align_bytes=64, name="x_codes")
             x_scales = quant.tile([P, PAIR, PASSES, P], U8, align_bytes=64, name="x_scales")
-            nc.vector.quantize_mx(
-                out=x_codes[:].rearrange("p j g r -> p (j g r)").bitcast(FP8X4),
-                scales=x_scales[:].rearrange("p j g r -> p (j g r)"),
-                in_=groupeds[pair][:].rearrange("p j g r t -> p (j g r t)"),
-            )
+            for j in range(PAIR):
+                nc.vector.quantize_mx(
+                    out=x_codes[:, j].rearrange("p g r -> p (g r)").bitcast(FP8X4),
+                    scales=x_scales[:, j].rearrange("p g r -> p (g r)"),
+                    in_=groupeds[pair][:, j].rearrange("p g r t -> p (g r t)"),
+                )
             codes[pair] = (x_codes, x_scales)
 
         def multiply(pair):
@@ -157,8 +158,11 @@ def tile_modelnew_kernel(tc, x, weight_words, weight_scales, bias, gamma, beta, 
                     accum_out=row_sum[:, j : j + 1],
                 )
                 ts[pair].append(t)
+            row_sums[pair] = row_sum
+
+        def negate_mean(pair):
             neg_mean = stats.tile([P, PAIR], F32, name="neg_mean")
-            nc.vector.tensor_scalar(out=neg_mean[:], in0=row_sum[:], scalar1=-1.0 / N, scalar2=None, op0=ALU.mult)
+            nc.vector.tensor_scalar(out=neg_mean[:], in0=row_sums[pair][:], scalar1=-1.0 / N, scalar2=None, op0=ALU.mult)
             neg_means[pair] = neg_mean
 
         def variance(pair):
@@ -187,8 +191,7 @@ def tile_modelnew_kernel(tc, x, weight_words, weight_scales, bias, gamma, beta, 
                 )
                 centreds[pair].append(centred)
 
-        def normalise_and_max(pair):
-            neg_max = stats.tile([P, PAIR], F32, name="neg_max")
+        def normalise(pair):
             zs[pair] = []
             for j in range(PAIR):
                 z = work.tile([P, N], F32, name="z")
@@ -196,8 +199,14 @@ def tile_modelnew_kernel(tc, x, weight_words, weight_scales, bias, gamma, beta, 
                     out=z[:], in0=centreds[pair][j][:], scalar=rstds[pair][:, j : j + 1], in1=shift[:],
                     op0=ALU.mult, op1=ALU.add,
                 )
-                nc.vector.tensor_reduce(out=neg_max[:, j : j + 1], in_=z[:], axis=AXIS.X, op=ALU.max, negate=True)
                 zs[pair].append(z)
+
+        def row_max(pair):
+            neg_max = stats.tile([P, PAIR], F32, name="neg_max")
+            for j in range(PAIR):
+                nc.vector.tensor_reduce(
+                    out=neg_max[:, j : j + 1], in_=zs[pair][j][:], axis=AXIS.X, op=ALU.max, negate=True
+                )
             neg_maxs[pair] = neg_max
 
         def exponentials(pair):
@@ -228,16 +237,17 @@ def tile_modelnew_kernel(tc, x, weight_words, weight_scales, bias, gamma, beta, 
             if 0 <= pair < PAIRS:
                 stage(pair)
 
-        with tc.manual_schedule():
-            for step in range(-3, PAIRS + 2):
-                run(quantise_x, step + 1)
-                run(multiply, step + 1)
-                run(divide_and_store, step - 2)
-                run(regroup_x, step + 2)
-                run(add_bias, step)
-                run(variance, step)
-                run(normalise_and_max, step - 1)
-                run(exponentials, step - 1)
-                run(centre_and_gain, step)
-                run(invert_sums, step - 1)
-                run(transpose_x, step + 3)
+        for step in range(-3, PAIRS + 2):
+            run(regroup_x, step + 2)
+            run(quantise_x, step + 1)
+            run(multiply, step + 1)
+            run(transpose_x, step + 3)
+            run(invert_sums, step - 2)
+            run(divide_and_store, step - 2)
+            run(add_bias, step)
+            run(normalise, step - 1)
+            run(negate_mean, step)
+            run(variance, step)
+            run(row_max, step - 1)
+            run(exponentials, step - 1)
+            run(centre_and_gain, step)

@@ -237,17 +237,18 @@ def tile_modelnew_kernel(tc, x, weight_words, weight_scales, bias, gamma, beta, 
             if 0 <= pair < PAIRS:
                 stage(pair)
 
-        for step in range(-3, PAIRS + 2):
-            run(regroup_x, step + 2)
-            run(quantise_x, step + 1)
-            run(multiply, step + 1)
-            run(transpose_x, step + 3)
-            run(invert_sums, step - 2)
-            run(divide_and_store, step - 2)
-            run(add_bias, step)
-            run(normalise, step - 1)
-            run(negate_mean, step)
-            run(variance, step)
-            run(row_max, step - 1)
-            run(exponentials, step - 1)
-            run(centre_and_gain, step)
+        with tc.manual_schedule():
+            for step in range(-2, PAIRS + 4):
+                run(regroup_x, step + 1)
+                run(transpose_x, step + 2)
+                run(invert_sums, step - 4)
+                run(add_bias, step)
+                run(normalise, step - 2)
+                run(negate_mean, step)
+                run(quantise_x, step + 1)
+                run(multiply, step + 1)
+                run(variance, step - 1)
+                run(row_max, step - 2)
+                run(exponentials, step - 3)
+                run(centre_and_gain, step)
+                run(divide_and_store, step - 4)

@@ -27,17 +27,25 @@ PAIR = 2
 PAIRS = ROW_TILES // PAIR
 
 
+def Z_ON_VECTOR(i):
+    return True
+
+
+def D_ON_GPSIMD(i):
+    return False
+
+
 def tile_modelnew_kernel(tc, x, weight_words, weight_scales, bias, gamma, beta, scale, out):
     nc = tc.nc
     with ExitStack() as ctx:
         const = ctx.enter_context(tc.tile_pool(name="const", bufs=1))
         xin = ctx.enter_context(tc.tile_pool(name="xin", bufs=ROW_TILES))
         quant = ctx.enter_context(tc.tile_pool(name="quant", bufs=3))
-        work = ctx.enter_context(tc.tile_pool(name="work", bufs=6))
-        stats = ctx.enter_context(tc.tile_pool(name="stats", bufs=4))
+        work = ctx.enter_context(tc.tile_pool(name="work", bufs=4))
+        stats = ctx.enter_context(tc.tile_pool(name="stats", bufs=8))
         psum_const = ctx.enter_context(tc.psum_pool(name="psum_const", bufs=1))
-        psum_xt = ctx.enter_context(tc.psum_pool(name="psum_xt", bufs=2))
-        psum_acc = ctx.enter_context(tc.psum_pool(name="psum_acc", bufs=4))
+        psum_xt = ctx.enter_context(tc.psum_pool(name="psum_xt", bufs=3))
+        psum_acc = ctx.enter_context(tc.psum_pool(name="psum_acc", bufs=3))
 
         w_scales = const.tile([P, PASSES, N], U8, align_bytes=64)
         nc.vector.memset(w_scales[:].bitcast(I32), 0)
@@ -45,7 +53,7 @@ def tile_modelnew_kernel(tc, x, weight_words, weight_scales, bias, gamma, beta, 
         nc.vector.memset(vec_rows[:], 0.0)
         ones = const.tile([P, P], BF16)
         nc.vector.memset(ones[:], 1.0)
-        neg_half = const.tile([P, PAIR], F32)
+        neg_half = const.tile([P, 1], F32)
         nc.vector.memset(neg_half[:], -0.5)
         ident = const.tile([P, P], F32)
         make_identity(nc, ident[:])
@@ -94,161 +102,169 @@ def tile_modelnew_kernel(tc, x, weight_words, weight_scales, bias, gamma, beta, 
             out=shift[:], lhsT=scale_col[:, 0:1].to_broadcast([P, P]), rhs=vec_rows[:, 2, :], start=True, stop=True
         )
 
+        shift_all = const.tile([P, N], F32)
+        nc.scalar.copy(out=shift_all[:], in_=shift[:])
+
         xts, groupeds, codes, accs, ts, centreds, zs, es = {}, {}, {}, {}, {}, {}, {}, {}
         row_sums, neg_means, rstds, neg_maxs, exp_sums, inv_sums = {}, {}, {}, {}, {}, {}
 
-        def transpose_x(pair):
-            xts[pair] = []
-            for j in range(PAIR):
-                x_words = x_tiles[pair * PAIR + j][:].bitcast(F32)
-                xt = psum_xt.tile([P, PASSES, HALVES, P], F32, name="xt")
-                for g in range(PASSES):
-                    for u in range(HALVES):
-                        nc.tensor.transpose(
-                            xt[:, g, u, :],
-                            x_words[:, (K_PASS // 2) * g + u : (K_PASS // 2) * (g + 1) : HALVES],
-                            ident[:],
-                        )
-                xts[pair].append(xt)
+        def z_on_vector(i):
+            return Z_ON_VECTOR(i)
 
-        def regroup_x(pair):
-            grouped = quant.tile([P, PAIR, PASSES, P, PACK], BF16, align_bytes=64, name="grouped")
-            for j in range(PAIR):
-                nc.scalar.copy(
-                    out=grouped[:, j].bitcast(F32),
-                    in_=xts[pair][j][:].rearrange("p g u r -> p g r u"),
-                )
-            groupeds[pair] = grouped
+        def d_on_gpsimd(i):
+            return D_ON_GPSIMD(i)
 
-        def quantise_x(pair):
-            x_codes = quant.tile([P, PAIR, PASSES, P], U32, align_bytes=64, name="x_codes")
-            x_scales = quant.tile([P, PAIR, PASSES, P], U8, align_bytes=64, name="x_scales")
-            for j in range(PAIR):
-                nc.vector.quantize_mx(
-                    out=x_codes[:, j].rearrange("p g r -> p (g r)").bitcast(FP8X4),
-                    scales=x_scales[:, j].rearrange("p g r -> p (g r)"),
-                    in_=groupeds[pair][:, j].rearrange("p g r t -> p (g r t)"),
-                )
-            codes[pair] = (x_codes, x_scales)
-
-        def multiply(pair):
-            x_codes, x_scales = codes[pair]
-            accs[pair] = []
-            for j in range(PAIR):
-                acc = psum_acc.tile([P, N], F32, name="acc")
-                for g in range(PASSES):
-                    nc.tensor.matmul_mx(
-                        out=acc[:],
-                        lhsT=x_codes[:, j, g, :].bitcast(FP8X4),
-                        lhsT_scale=x_scales[:, j, g, :],
-                        rhs=w_codes[:, g, :].bitcast(FP8X4),
-                        rhs_scale=w_scales[:, g, :],
-                        start=(g == 0),
-                        stop=(g == PASSES - 1),
+        def transpose_x(i):
+            x_words = x_tiles[i][:].bitcast(F32)
+            xt = psum_xt.tile([P, PASSES, HALVES, P], F32, name="xt")
+            for g in range(PASSES):
+                for u in range(HALVES):
+                    nc.tensor.transpose(
+                        xt[:, g, u, :],
+                        x_words[:, (K_PASS // 2) * g + u : (K_PASS // 2) * (g + 1) : HALVES],
+                        ident[:],
                     )
-                accs[pair].append(acc)
+            xts[i] = xt
 
-        def add_bias(pair):
-            row_sum = stats.tile([P, PAIR], F32, name="row_sum")
-            ts[pair] = []
-            for j in range(PAIR):
-                t = work.tile([P, N], F32, name="t")
-                nc.vector.scalar_tensor_tensor(
-                    out=t[:], in0=accs[pair][j][:], scalar=1.0, in1=bias_all[:], op0=ALU.mult, op1=ALU.add,
-                    accum_out=row_sum[:, j : j + 1],
-                )
-                ts[pair].append(t)
-            row_sums[pair] = row_sum
+        def regroup_x(i):
+            grouped = quant.tile([P, PASSES, P, PACK], BF16, align_bytes=64, name="grouped")
+            nc.scalar.copy(out=grouped[:].bitcast(F32), in_=xts[i][:].rearrange("p g u r -> p g r u"))
+            groupeds[i] = grouped
 
-        def negate_mean(pair):
-            neg_mean = stats.tile([P, PAIR], F32, name="neg_mean")
-            nc.vector.tensor_scalar(out=neg_mean[:], in0=row_sums[pair][:], scalar1=-1.0 / N, scalar2=None, op0=ALU.mult)
-            neg_means[pair] = neg_mean
-
-        def variance(pair):
-            sq_sum = stats.tile([P, PAIR], F32, name="sq_sum")
-            for j in range(PAIR):
-                squares = work.tile([P, N], F32, name="squares")
-                nc.scalar.activation(
-                    out=squares[:], in_=ts[pair][j][:], func=ACT.Square, bias=neg_means[pair][:, j : j + 1],
-                    scale=1.0, accum_out=sq_sum[:, j : j + 1],
-                )
-            var_eps = stats.tile([P, PAIR], F32, name="var_eps")
-            nc.gpsimd.tensor_scalar(
-                out=var_eps[:], in0=sq_sum[:], scalar1=1.0 / N, scalar2=EPS, op0=ALU.mult, op1=ALU.add
+        def quantise_x(i):
+            x_codes = quant.tile([P, PASSES, P], U32, align_bytes=64, name="x_codes")
+            x_scales = quant.tile([P, PASSES, P], U8, align_bytes=64, name="x_scales")
+            nc.vector.quantize_mx(
+                out=x_codes[:].rearrange("p g r -> p (g r)").bitcast(FP8X4),
+                scales=x_scales[:].rearrange("p g r -> p (g r)"),
+                in_=groupeds[i][:].rearrange("p g r t -> p (g r t)"),
             )
-            rstd = stats.tile([P, PAIR], F32, name="rstd")
-            nc.gpsimd.tensor_tensor(out=rstd[:], in0=var_eps[:], in1=neg_half[:], op=ALU.pow)
-            rstds[pair] = rstd
+            codes[i] = (x_codes, x_scales)
 
-        def centre_and_gain(pair):
-            centreds[pair] = []
-            for j in range(PAIR):
-                centred = work.tile([P, N], F32, name="centred")
-                nc.vector.scalar_tensor_tensor(
-                    out=centred[:], in0=ts[pair][j][:], scalar=neg_means[pair][:, j : j + 1], in1=gain[:],
-                    op0=ALU.add, op1=ALU.mult,
+        def multiply(i):
+            x_codes, x_scales = codes[i]
+            acc = psum_acc.tile([P, N], F32, name="acc")
+            for g in range(PASSES):
+                nc.tensor.matmul_mx(
+                    out=acc[:],
+                    lhsT=x_codes[:, g, :].bitcast(FP8X4),
+                    lhsT_scale=x_scales[:, g, :],
+                    rhs=w_codes[:, g, :].bitcast(FP8X4),
+                    rhs_scale=w_scales[:, g, :],
+                    start=(g == 0),
+                    stop=(g == PASSES - 1),
                 )
-                centreds[pair].append(centred)
+            accs[i] = acc
 
-        def normalise(pair):
-            zs[pair] = []
-            for j in range(PAIR):
+        def add_bias(i):
+            row_sum = stats.tile([P, 1], F32, name="row_sum")
+            t = work.tile([P, N], F32, name="t")
+            nc.vector.scalar_tensor_tensor(
+                out=t[:], in0=accs[i][:], scalar=1.0, in1=bias_all[:], op0=ALU.mult, op1=ALU.add,
+                accum_out=row_sum[:],
+            )
+            ts[i] = t
+            row_sums[i] = row_sum
+
+        def negate_mean(i):
+            neg_mean = stats.tile([P, 1], F32, name="neg_mean")
+            nc.scalar.activation(out=neg_mean[:], in_=row_sums[i][:], func=ACT.Copy, scale=-1.0 / N)
+            neg_means[i] = neg_mean
+
+        def squares_sum(i):
+            sq_sum = stats.tile([P, 1], F32, name="sq_sum")
+            squares = work.tile([P, N], F32, name="squares")
+            nc.scalar.activation(
+                out=squares[:], in_=ts[i][:], func=ACT.Square, bias=neg_means[i][:], scale=1.0, accum_out=sq_sum[:],
+            )
+            rstds[i] = sq_sum
+
+        def inverse_deviation(i):
+            var_eps = stats.tile([P, 1], F32, name="var_eps")
+            nc.gpsimd.tensor_scalar(
+                out=var_eps[:], in0=rstds[i][:], scalar1=1.0 / N, scalar2=EPS, op0=ALU.mult, op1=ALU.add
+            )
+            rstd = stats.tile([P, 1], F32, name="rstd")
+            nc.gpsimd.tensor_tensor(out=rstd[:], in0=var_eps[:], in1=neg_half[:], op=ALU.pow)
+            rstds[i] = rstd
+
+        def centre_and_gain(i):
+            centred = work.tile([P, N], F32, name="centred")
+            nc.vector.scalar_tensor_tensor(
+                out=centred[:], in0=ts[i][:], scalar=neg_means[i][:], in1=gain[:], op0=ALU.add, op1=ALU.mult,
+            )
+            centreds[i] = centred
+
+        def normalise_vector(i):
+            if z_on_vector(i):
                 z = work.tile([P, N], F32, name="z")
                 nc.vector.scalar_tensor_tensor(
-                    out=z[:], in0=centreds[pair][j][:], scalar=rstds[pair][:, j : j + 1], in1=shift[:],
-                    op0=ALU.mult, op1=ALU.add,
+                    out=z[:], in0=centreds[i][:], scalar=rstds[i][:], in1=shift[:], op0=ALU.mult, op1=ALU.add,
                 )
-                zs[pair].append(z)
+                zs[i] = z
 
-        def row_max(pair):
-            neg_max = stats.tile([P, PAIR], F32, name="neg_max")
-            for j in range(PAIR):
-                nc.vector.tensor_reduce(
-                    out=neg_max[:, j : j + 1], in_=zs[pair][j][:], axis=AXIS.X, op=ALU.max, negate=True
+        def normalise_gpsimd(i):
+            if not z_on_vector(i):
+                scaled = work.tile([P, N], F32, name="scaled")
+                nc.gpsimd.tensor_scalar(
+                    out=scaled[:], in0=centreds[i][:], scalar1=rstds[i][:], scalar2=0.0, op0=ALU.mult, op1=ALU.add
                 )
-            neg_maxs[pair] = neg_max
+                z = work.tile([P, N], F32, name="z")
+                nc.gpsimd.tensor_tensor(out=z[:], in0=scaled[:], in1=shift_all[:], op=ALU.add)
+                zs[i] = z
 
-        def exponentials(pair):
-            exp_sum = stats.tile([P, PAIR], F32, name="exp_sum")
-            es[pair] = []
-            for j in range(PAIR):
-                e = work.tile([P, N], F32, name="e")
-                nc.scalar.activation(
-                    out=e[:], in_=zs[pair][j][:], func=ACT.Exp, bias=neg_maxs[pair][:, j : j + 1], scale=1.0,
-                    accum_out=exp_sum[:, j : j + 1],
-                )
-                es[pair].append(e)
-            exp_sums[pair] = exp_sum
+        def row_max(i):
+            neg_max = stats.tile([P, 1], F32, name="neg_max")
+            nc.vector.tensor_reduce(out=neg_max[:], in_=zs[i][:], axis=AXIS.X, op=ALU.max, negate=True)
+            neg_maxs[i] = neg_max
 
-        def invert_sums(pair):
-            inv_sum = stats.tile([P, PAIR], F32, name="inv_sum")
-            nc.vector.reciprocal(out=inv_sum[:], in_=exp_sums[pair][:])
-            inv_sums[pair] = inv_sum
+        def exponentials(i):
+            exp_sum = stats.tile([P, 1], F32, name="exp_sum")
+            e = work.tile([P, N], F32, name="e")
+            nc.scalar.activation(
+                out=e[:], in_=zs[i][:], func=ACT.Exp, bias=neg_maxs[i][:], scale=1.0, accum_out=exp_sum[:],
+            )
+            es[i] = e
+            exp_sums[i] = exp_sum
 
-        def divide_and_store(pair):
-            for j in range(PAIR):
-                row0 = (pair * PAIR + j) * P
+        def invert_sum(i):
+            inv_sum = stats.tile([P, 1], F32, name="inv_sum")
+            nc.vector.reciprocal(out=inv_sum[:], in_=exp_sums[i][:])
+            inv_sums[i] = inv_sum
+
+        def divide_scalar(i):
+            if not d_on_gpsimd(i):
                 probs = work.tile([P, N], F32, name="probs")
-                nc.scalar.activation(out=probs[:], in_=es[pair][j][:], func=ACT.Copy, scale=inv_sums[pair][:, j : j + 1])
-                nc.sync.dma_start(out=out[row0 : row0 + P, :], in_=probs[:])
+                nc.scalar.activation(out=probs[:], in_=es[i][:], func=ACT.Copy, scale=inv_sums[i][:])
+                nc.sync.dma_start(out=out[i * P : (i + 1) * P, :], in_=probs[:])
 
-        def run(stage, pair):
-            if 0 <= pair < PAIRS:
-                stage(pair)
+        def divide_gpsimd(i):
+            if d_on_gpsimd(i):
+                probs = work.tile([P, N], F32, name="probs")
+                nc.gpsimd.tensor_scalar(
+                    out=probs[:], in0=es[i][:], scalar1=inv_sums[i][:], scalar2=0.0, op0=ALU.mult, op1=ALU.add
+                )
+                nc.sync.dma_start(out=out[i * P : (i + 1) * P, :], in_=probs[:])
+
+        def run(stage, i):
+            if 0 <= i < ROW_TILES:
+                stage(i)
 
         with tc.manual_schedule():
-            for step in range(-2, PAIRS + 4):
-                run(regroup_x, step + 1)
-                run(transpose_x, step + 2)
-                run(invert_sums, step - 4)
+            for step in range(-4, ROW_TILES + 6):
+                run(transpose_x, step + 4)
+                run(regroup_x, step + 3)
+                run(invert_sum, step - 5)
                 run(add_bias, step)
-                run(normalise, step - 2)
-                run(negate_mean, step)
-                run(quantise_x, step + 1)
                 run(multiply, step + 1)
-                run(variance, step - 1)
-                run(row_max, step - 2)
-                run(exponentials, step - 3)
-                run(centre_and_gain, step)
-                run(divide_and_store, step - 4)
+                run(normalise_gpsimd, step - 2)
+                run(squares_sum, step - 1)
+                run(row_max, step - 3)
+                run(quantise_x, step + 2)
+                run(exponentials, step - 4)
+                run(centre_and_gain, step - 1)
+                run(normalise_vector, step - 2)
+                run(divide_scalar, step - 5)
+                run(divide_gpsimd, step - 5)
+                run(negate_mean, step)
+                run(inverse_deviation, step - 1)

@@ -181,9 +181,7 @@ def tile_modelnew_kernel(tc, x, weight_words, weight_scales, bias, gamma, beta, 
 
         def inverse_deviation(i):
             var_eps = stats.tile([P, 1], F32, name="var_eps")
-            nc.gpsimd.tensor_scalar(
-                out=var_eps[:], in0=rstds[i][:], scalar1=1.0 / N, scalar2=EPS, op0=ALU.mult, op1=ALU.add
-            )
+            nc.scalar.activation(out=var_eps[:], in_=rstds[i][:], func=ACT.Copy, scale=1.0 / N, bias=EPS)
             rstd = stats.tile([P, 1], F32, name="rstd")
             nc.gpsimd.tensor_tensor(out=rstd[:], in0=var_eps[:], in1=neg_half[:], op=ALU.pow)
             rstds[i] = rstd

@@ -27,12 +27,33 @@ PAIR = 2
 PAIRS = ROW_TILES // PAIR
 
 
-def Z_ON_VECTOR(i):
-    return True
+GROUPS = [[i] for i in range(ROW_TILES)]
+DIVIDE_ON_VECTOR_EVERY = 4
 
 
-def D_ON_GPSIMD(i):
-    return False
+def TILE_STAGES(transpose_x, regroup_x, multiply, add_bias, negate_mean, squares_sum, centre_and_gain, normalise,
+                exponentials, divide_and_store):
+    return [
+        (transpose_x, -4, 0, 0),
+        (regroup_x, -3, 0, 1),
+        (add_bias, 0, 0, 3),
+        (multiply, -1, 0, 4),
+        (negate_mean, 0, 0, 14),
+        (squares_sum, 1, 0, 6),
+        (centre_and_gain, 1, 0, 10),
+        (normalise, 2, 0, 11),
+        (exponentials, 4, 0, 9),
+        (divide_and_store, 5, 0, 12),
+    ]
+
+
+def GROUP_STAGES(quantise_x, inverse_deviation, row_max, invert_sums):
+    return [
+        (quantise_x, -2, 0, 8),
+        (inverse_deviation, 1, 0, 15),
+        (row_max, 3, 0, 7),
+        (invert_sums, 5, 0, 2),
+    ]
 
 
 def tile_modelnew_kernel(tc, x, weight_words, weight_scales, bias, gamma, beta, scale, out):
@@ -41,7 +62,8 @@ def tile_modelnew_kernel(tc, x, weight_words, weight_scales, bias, gamma, beta, 
         const = ctx.enter_context(tc.tile_pool(name="const", bufs=1))
         xin = ctx.enter_context(tc.tile_pool(name="xin", bufs=ROW_TILES))
         quant = ctx.enter_context(tc.tile_pool(name="quant", bufs=3))
-        work = ctx.enter_context(tc.tile_pool(name="work", bufs=4))
+        work = ctx.enter_context(tc.tile_pool(name="work", bufs=6))
+        pairs = ctx.enter_context(tc.tile_pool(name="pairs", bufs=4))
         stats = ctx.enter_context(tc.tile_pool(name="stats", bufs=8))
         psum_const = ctx.enter_context(tc.psum_pool(name="psum_const", bufs=1))
         psum_xt = ctx.enter_context(tc.psum_pool(name="psum_xt", bufs=3))
@@ -53,7 +75,7 @@ def tile_modelnew_kernel(tc, x, weight_words, weight_scales, bias, gamma, beta, 
         nc.vector.memset(vec_rows[:], 0.0)
         ones = const.tile([P, P], BF16)
         nc.vector.memset(ones[:], 1.0)
-        neg_half = const.tile([P, 1], F32)
+        neg_half = const.tile([P, PAIR], F32)
         nc.vector.memset(neg_half[:], -0.5)
         ident = const.tile([P, P], F32)
         make_identity(nc, ident[:])
@@ -102,17 +124,15 @@ def tile_modelnew_kernel(tc, x, weight_words, weight_scales, bias, gamma, beta, 
             out=shift[:], lhsT=scale_col[:, 0:1].to_broadcast([P, P]), rhs=vec_rows[:, 2, :], start=True, stop=True
         )
 
-        shift_all = const.tile([P, N], F32)
-        nc.scalar.copy(out=shift_all[:], in_=shift[:])
+        groups = GROUPS
+        group_of, slot_of = {}, {}
+        for index, members in enumerate(groups):
+            for slot, i in enumerate(members):
+                group_of[i] = index
+                slot_of[i] = slot
 
-        xts, groupeds, codes, accs, ts, centreds, zs, es = {}, {}, {}, {}, {}, {}, {}, {}
-        row_sums, neg_means, rstds, neg_maxs, exp_sums, inv_sums = {}, {}, {}, {}, {}, {}
-
-        def z_on_vector(i):
-            return Z_ON_VECTOR(i)
-
-        def d_on_gpsimd(i):
-            return D_ON_GPSIMD(i)
+        xts, accs, ts, centreds, es, neg_means, row_sums = {}, {}, {}, {}, {}, {}, {}
+        groupeds, codes, zs, sq_sums, rstds, neg_maxs, exp_sums, inv_sums = {}, {}, {}, {}, {}, {}, {}, {}
 
         def transpose_x(i):
             x_words = x_tiles[i][:].bitcast(F32)
@@ -127,28 +147,32 @@ def tile_modelnew_kernel(tc, x, weight_words, weight_scales, bias, gamma, beta, 
             xts[i] = xt
 
         def regroup_x(i):
-            grouped = quant.tile([P, PASSES, P, PACK], BF16, align_bytes=64, name="grouped")
-            nc.scalar.copy(out=grouped[:].bitcast(F32), in_=xts[i][:].rearrange("p g u r -> p g r u"))
-            groupeds[i] = grouped
+            q, j = group_of[i], slot_of[i]
+            if j == 0:
+                grouped = quant.tile([P, PAIR, PASSES, P, PACK], BF16, align_bytes=64, name="grouped")
+                groupeds[q] = grouped
+            nc.scalar.copy(out=groupeds[q][:, j].bitcast(F32), in_=xts[i][:].rearrange("p g u r -> p g r u"))
 
-        def quantise_x(i):
-            x_codes = quant.tile([P, PASSES, P], U32, align_bytes=64, name="x_codes")
-            x_scales = quant.tile([P, PASSES, P], U8, align_bytes=64, name="x_scales")
+        def quantise_x(q):
+            n = len(groups[q])
+            x_codes = quant.tile([P, PAIR, PASSES, P], U32, align_bytes=64, name="x_codes")
+            x_scales = quant.tile([P, PAIR, PASSES, P], U8, align_bytes=64, name="x_scales")
             nc.vector.quantize_mx(
-                out=x_codes[:].rearrange("p g r -> p (g r)").bitcast(FP8X4),
-                scales=x_scales[:].rearrange("p g r -> p (g r)"),
-                in_=groupeds[i][:].rearrange("p g r t -> p (g r t)"),
+                out=x_codes[:, 0:n].rearrange("p j g r -> p (j g r)").bitcast(FP8X4),
+                scales=x_scales[:, 0:n].rearrange("p j g r -> p (j g r)"),
+                in_=groupeds[q][:, 0:n].rearrange("p j g r t -> p (j g r t)"),
             )
-            codes[i] = (x_codes, x_scales)
+            codes[q] = (x_codes, x_scales)
 
         def multiply(i):
-            x_codes, x_scales = codes[i]
+            x_codes, x_scales = codes[group_of[i]]
+            j = slot_of[i]
             acc = psum_acc.tile([P, N], F32, name="acc")
             for g in range(PASSES):
                 nc.tensor.matmul_mx(
                     out=acc[:],
-                    lhsT=x_codes[:, g, :].bitcast(FP8X4),
-                    lhsT_scale=x_scales[:, g, :],
+                    lhsT=x_codes[:, j, g, :].bitcast(FP8X4),
+                    lhsT_scale=x_scales[:, j, g, :],
                     rhs=w_codes[:, g, :].bitcast(FP8X4),
                     rhs_scale=w_scales[:, g, :],
                     start=(g == 0),
@@ -172,19 +196,23 @@ def tile_modelnew_kernel(tc, x, weight_words, weight_scales, bias, gamma, beta, 
             neg_means[i] = neg_mean
 
         def squares_sum(i):
-            sq_sum = stats.tile([P, 1], F32, name="sq_sum")
+            q, j = group_of[i], slot_of[i]
+            if j == 0:
+                sq_sum = stats.tile([P, PAIR], F32, name="sq_sum")
+                sq_sums[q] = sq_sum
             squares = work.tile([P, N], F32, name="squares")
             nc.scalar.activation(
-                out=squares[:], in_=ts[i][:], func=ACT.Square, bias=neg_means[i][:], scale=1.0, accum_out=sq_sum[:],
+                out=squares[:], in_=ts[i][:], func=ACT.Square, bias=neg_means[i][:], scale=1.0,
+                accum_out=sq_sums[q][:, j : j + 1],
             )
-            rstds[i] = sq_sum
 
-        def inverse_deviation(i):
-            var_eps = stats.tile([P, 1], F32, name="var_eps")
-            nc.scalar.activation(out=var_eps[:], in_=rstds[i][:], func=ACT.Copy, scale=1.0 / N, bias=EPS)
-            rstd = stats.tile([P, 1], F32, name="rstd")
-            nc.gpsimd.tensor_tensor(out=rstd[:], in0=var_eps[:], in1=neg_half[:], op=ALU.pow)
-            rstds[i] = rstd
+        def inverse_deviation(q):
+            n = len(groups[q])
+            var_eps = stats.tile([P, PAIR], F32, name="var_eps")
+            nc.scalar.activation(out=var_eps[:, 0:n], in_=sq_sums[q][:, 0:n], func=ACT.Copy, scale=1.0 / N, bias=EPS)
+            rstd = stats.tile([P, PAIR], F32, name="rstd")
+            nc.gpsimd.tensor_tensor(out=rstd[:, 0:n], in0=var_eps[:, 0:n], in1=neg_half[:, 0:n], op=ALU.pow)
+            rstds[q] = rstd
 
         def centre_and_gain(i):
             centred = work.tile([P, N], F32, name="centred")
@@ -193,76 +221,63 @@ def tile_modelnew_kernel(tc, x, weight_words, weight_scales, bias, gamma, beta, 
             )
             centreds[i] = centred
 
-        def normalise_vector(i):
-            if z_on_vector(i):
-                z = work.tile([P, N], F32, name="z")
-                nc.vector.scalar_tensor_tensor(
-                    out=z[:], in0=centreds[i][:], scalar=rstds[i][:], in1=shift[:], op0=ALU.mult, op1=ALU.add,
-                )
-                zs[i] = z
+        def normalise(i):
+            q, j = group_of[i], slot_of[i]
+            if j == 0:
+                z = pairs.tile([P, PAIR, N], F32, name="z")
+                zs[q] = z
+            nc.vector.scalar_tensor_tensor(
+                out=zs[q][:, j, :], in0=centreds[i][:], scalar=rstds[q][:, j : j + 1], in1=shift[:],
+                op0=ALU.mult, op1=ALU.add,
+            )
 
-        def normalise_gpsimd(i):
-            if not z_on_vector(i):
-                scaled = work.tile([P, N], F32, name="scaled")
-                nc.gpsimd.tensor_scalar(
-                    out=scaled[:], in0=centreds[i][:], scalar1=rstds[i][:], scalar2=0.0, op0=ALU.mult, op1=ALU.add
-                )
-                z = work.tile([P, N], F32, name="z")
-                nc.gpsimd.tensor_tensor(out=z[:], in0=scaled[:], in1=shift_all[:], op=ALU.add)
-                zs[i] = z
-
-        def row_max(i):
-            neg_max = stats.tile([P, 1], F32, name="neg_max")
-            nc.vector.tensor_reduce(out=neg_max[:], in_=zs[i][:], axis=AXIS.X, op=ALU.max, negate=True)
-            neg_maxs[i] = neg_max
+        def row_max(q):
+            n = len(groups[q])
+            neg_max = stats.tile([P, PAIR], F32, name="neg_max")
+            nc.vector.tensor_reduce(out=neg_max[:, 0:n], in_=zs[q][:, 0:n, :], axis=AXIS.X, op=ALU.max, negate=True)
+            neg_maxs[q] = neg_max
 
         def exponentials(i):
-            exp_sum = stats.tile([P, 1], F32, name="exp_sum")
+            q, j = group_of[i], slot_of[i]
+            if j == 0:
+                exp_sum = stats.tile([P, PAIR], F32, name="exp_sum")
+                exp_sums[q] = exp_sum
             e = work.tile([P, N], F32, name="e")
             nc.scalar.activation(
-                out=e[:], in_=zs[i][:], func=ACT.Exp, bias=neg_maxs[i][:], scale=1.0, accum_out=exp_sum[:],
+                out=e[:], in_=zs[q][:, j, :], func=ACT.Exp, bias=neg_maxs[q][:, j : j + 1], scale=1.0,
+                accum_out=exp_sums[q][:, j : j + 1],
             )
             es[i] = e
-            exp_sums[i] = exp_sum
 
-        def invert_sum(i):
-            inv_sum = stats.tile([P, 1], F32, name="inv_sum")
-            nc.vector.reciprocal(out=inv_sum[:], in_=exp_sums[i][:])
-            inv_sums[i] = inv_sum
+        def invert_sums(q):
+            n = len(groups[q])
+            inv_sum = stats.tile([P, PAIR], F32, name="inv_sum")
+            nc.vector.reciprocal(out=inv_sum[:, 0:n], in_=exp_sums[q][:, 0:n])
+            inv_sums[q] = inv_sum
 
-        def divide_scalar(i):
-            if not d_on_gpsimd(i):
-                probs = work.tile([P, N], F32, name="probs")
-                nc.scalar.activation(out=probs[:], in_=es[i][:], func=ACT.Copy, scale=inv_sums[i][:])
-                nc.sync.dma_start(out=out[i * P : (i + 1) * P, :], in_=probs[:])
-
-        def divide_gpsimd(i):
-            if d_on_gpsimd(i):
-                probs = work.tile([P, N], F32, name="probs")
-                nc.gpsimd.tensor_scalar(
-                    out=probs[:], in0=es[i][:], scalar1=inv_sums[i][:], scalar2=0.0, op0=ALU.mult, op1=ALU.add
+        def divide_and_store(i):
+            q, j = group_of[i], slot_of[i]
+            probs = work.tile([P, N], F32, name="probs")
+            if i % DIVIDE_ON_VECTOR_EVERY == DIVIDE_ON_VECTOR_EVERY - 1:
+                nc.vector.tensor_scalar(
+                    out=probs[:], in0=es[i][:], scalar1=inv_sums[q][:, j : j + 1], scalar2=None, op0=ALU.mult
                 )
-                nc.sync.dma_start(out=out[i * P : (i + 1) * P, :], in_=probs[:])
+            else:
+                nc.scalar.activation(out=probs[:], in_=es[i][:], func=ACT.Copy, scale=inv_sums[q][:, j : j + 1])
+            nc.sync.dma_start(out=out[i * P : (i + 1) * P, :], in_=probs[:])
 
-        def run(stage, i):
-            if 0 <= i < ROW_TILES:
-                stage(i)
-
+        tile_stages = TILE_STAGES(
+            transpose_x, regroup_x, multiply, add_bias, negate_mean, squares_sum, centre_and_gain, normalise,
+            exponentials, divide_and_store,
+        )
+        group_stages = GROUP_STAGES(quantise_x, inverse_deviation, row_max, invert_sums)
+        plan = []
+        for stage, offset, lag, place in tile_stages:
+            for i in range(ROW_TILES):
+                plan.append((i + offset + lag * (len(groups[group_of[i]]) - 1), place, i, stage))
+        for stage, offset, lag, place in group_stages:
+            for q, members in enumerate(groups):
+                plan.append((members[-1] + offset + lag * (len(members) - 1), place, q, stage))
         with tc.manual_schedule():
-            for step in range(-4, ROW_TILES + 6):
-                run(transpose_x, step + 4)
-                run(regroup_x, step + 3)
-                run(invert_sum, step - 5)
-                run(add_bias, step)
-                run(multiply, step + 1)
-                run(normalise_gpsimd, step - 2)
-                run(squares_sum, step - 1)
-                run(row_max, step - 3)
-                run(quantise_x, step + 2)
-                run(exponentials, step - 4)
-                run(centre_and_gain, step - 1)
-                run(normalise_vector, step - 2)
-                run(divide_scalar, step - 5)
-                run(divide_gpsimd, step - 5)
-                run(negate_mean, step)
-                run(inverse_deviation, step - 1)
+            for entry in sorted(plan, key=lambda item: item[0:3]):
+                entry[3](entry[2])

@@ -28,7 +28,7 @@ PAIRS = ROW_TILES // PAIR
 
 
 GROUPS = [[i] for i in range(ROW_TILES)]
-DIVIDE_ON_VECTOR_EVERY = 4
+TAIL_ON_VECTOR = 2
 
 
 def TILE_STAGES(transpose_x, regroup_x, multiply, add_bias, negate_mean, squares_sum, centre_and_gain, normalise,
@@ -77,6 +77,8 @@ def tile_modelnew_kernel(tc, x, weight_words, weight_scales, bias, gamma, beta, 
         nc.vector.memset(ones[:], 1.0)
         neg_half = const.tile([P, PAIR], F32)
         nc.vector.memset(neg_half[:], -0.5)
+        neg_one = const.tile([P, PAIR], F32)
+        nc.vector.memset(neg_one[:], -1.0)
         ident = const.tile([P, P], F32)
         make_identity(nc, ident[:])
         table_warm = const.tile([P, 1], F32)
@@ -192,7 +194,9 @@ def tile_modelnew_kernel(tc, x, weight_words, weight_scales, bias, gamma, beta, 
 
         def negate_mean(i):
             neg_mean = stats.tile([P, 1], F32, name="neg_mean")
-            nc.scalar.activation(out=neg_mean[:], in_=row_sums[i][:], func=ACT.Copy, scale=-1.0 / N)
+            nc.gpsimd.tensor_scalar(
+                out=neg_mean[:], in0=row_sums[i][:], scalar1=-1.0 / N, scalar2=0.0, op0=ALU.mult, op1=ALU.add
+            )
             neg_means[i] = neg_mean
 
         def squares_sum(i):
@@ -209,7 +213,9 @@ def tile_modelnew_kernel(tc, x, weight_words, weight_scales, bias, gamma, beta, 
         def inverse_deviation(q):
             n = len(groups[q])
             var_eps = stats.tile([P, PAIR], F32, name="var_eps")
-            nc.scalar.activation(out=var_eps[:, 0:n], in_=sq_sums[q][:, 0:n], func=ACT.Copy, scale=1.0 / N, bias=EPS)
+            nc.gpsimd.tensor_scalar(
+                out=var_eps[:, 0:n], in0=sq_sums[q][:, 0:n], scalar1=1.0 / N, scalar2=EPS, op0=ALU.mult, op1=ALU.add
+            )
             rstd = stats.tile([P, PAIR], F32, name="rstd")
             nc.gpsimd.tensor_tensor(out=rstd[:, 0:n], in0=var_eps[:, 0:n], in1=neg_half[:, 0:n], op=ALU.pow)
             rstds[q] = rstd
@@ -252,13 +258,16 @@ def tile_modelnew_kernel(tc, x, weight_words, weight_scales, bias, gamma, beta, 
         def invert_sums(q):
             n = len(groups[q])
             inv_sum = stats.tile([P, PAIR], F32, name="inv_sum")
-            nc.vector.reciprocal(out=inv_sum[:, 0:n], in_=exp_sums[q][:, 0:n])
+            if groups[q][0] >= ROW_TILES - TAIL_ON_VECTOR:
+                nc.vector.reciprocal(out=inv_sum[:, 0:n], in_=exp_sums[q][:, 0:n])
+            else:
+                nc.gpsimd.tensor_tensor(out=inv_sum[:, 0:n], in0=exp_sums[q][:, 0:n], in1=neg_one[:, 0:n], op=ALU.pow)
             inv_sums[q] = inv_sum
 
         def divide_and_store(i):
             q, j = group_of[i], slot_of[i]
             probs = work.tile([P, N], F32, name="probs")
-            if i % DIVIDE_ON_VECTOR_EVERY == DIVIDE_ON_VECTOR_EVERY - 1:
+            if i >= ROW_TILES - TAIL_ON_VECTOR:
                 nc.vector.tensor_scalar(
                     out=probs[:], in0=es[i][:], scalar1=inv_sums[q][:, j : j + 1], scalar2=None, op0=ALU.mult
                 )

@@ -23,37 +23,9 @@ K_PASS = P * PACK
 PASSES = K // K_PASS
 HALVES = 2
 ROW_TILES = M // P
-PAIR = 2
-PAIRS = ROW_TILES // PAIR
-
-
-GROUPS = [[i] for i in range(ROW_TILES)]
-TAIL_ON_VECTOR = 2
-
-
-def TILE_STAGES(transpose_x, regroup_x, multiply, add_bias, negate_mean, squares_sum, centre_and_gain, normalise,
-                exponentials, divide_and_store):
-    return [
-        (transpose_x, -4, 0, 0),
-        (regroup_x, -3, 0, 1),
-        (add_bias, 0, 0, 3),
-        (multiply, -1, 0, 4),
-        (negate_mean, 0, 0, 14),
-        (squares_sum, 1, 0, 6),
-        (centre_and_gain, 1, 0, 10),
-        (normalise, 2, 0, 11),
-        (exponentials, 4, 0, 9),
-        (divide_and_store, 5, 0, 12),
-    ]
-
-
-def GROUP_STAGES(quantise_x, inverse_deviation, row_max, invert_sums):
-    return [
-        (quantise_x, -2, 0, 8),
-        (inverse_deviation, 1, 0, 15),
-        (row_max, 3, 0, 7),
-        (invert_sums, 5, 0, 2),
-    ]
+TAIL_TILES = 2
+LEAD = 4
+HEAD_TILES = 2
 
 
 def tile_modelnew_kernel(tc, x, weight_words, weight_scales, bias, gamma, beta, scale, out):
@@ -62,38 +34,42 @@ def tile_modelnew_kernel(tc, x, weight_words, weight_scales, bias, gamma, beta, 
         const = ctx.enter_context(tc.tile_pool(name="const", bufs=1))
         xin = ctx.enter_context(tc.tile_pool(name="xin", bufs=ROW_TILES))
         quant = ctx.enter_context(tc.tile_pool(name="quant", bufs=3))
-        work = ctx.enter_context(tc.tile_pool(name="work", bufs=6))
-        pairs = ctx.enter_context(tc.tile_pool(name="pairs", bufs=4))
+        work = ctx.enter_context(tc.tile_pool(name="work", bufs=4))
         stats = ctx.enter_context(tc.tile_pool(name="stats", bufs=8))
         psum_const = ctx.enter_context(tc.psum_pool(name="psum_const", bufs=1))
         psum_xt = ctx.enter_context(tc.psum_pool(name="psum_xt", bufs=3))
         psum_acc = ctx.enter_context(tc.psum_pool(name="psum_acc", bufs=3))
+        ctx.enter_context(tc.manual_schedule())
 
-        w_scales = const.tile([P, PASSES, N], U8, align_bytes=64)
-        nc.vector.memset(w_scales[:].bitcast(I32), 0)
         vec_rows = const.tile([P, 3, N], BF16)
         nc.vector.memset(vec_rows[:], 0.0)
+        scale_col = const.tile([P, 1], BF16)
+        nc.scalar.dma_start(out=scale_col[:], in_=scale.partition_broadcast(P))
+        nc.scalar.dma_start(out=vec_rows[0:1, 0, :], in_=bias.unsqueeze(0))
+        nc.scalar.dma_start(out=vec_rows[0:1, 1, :], in_=gamma.unsqueeze(0))
+        nc.scalar.dma_start(out=vec_rows[0:1, 2, :], in_=beta.unsqueeze(0))
+        w_scales = const.tile([P, PASSES, N], U8, align_bytes=64)
+        nc.vector.memset(w_scales[:].bitcast(I32), 0)
         ones = const.tile([P, P], BF16)
         nc.vector.memset(ones[:], 1.0)
-        neg_half = const.tile([P, PAIR], F32)
+        neg_half = const.tile([P, 1], F32)
         nc.vector.memset(neg_half[:], -0.5)
-        neg_one = const.tile([P, PAIR], F32)
+        neg_one = const.tile([P, 1], F32)
         nc.vector.memset(neg_one[:], -1.0)
         ident = const.tile([P, P], F32)
         make_identity(nc, ident[:])
         table_warm = const.tile([P, 1], F32)
-        nc.scalar.activation(out=table_warm[:], in_=neg_half[:, 0:1], func=ACT.Exp)
+        nc.scalar.activation(out=table_warm[:], in_=neg_half[:], func=ACT.Exp)
 
         x_tiles = []
         for i in range(ROW_TILES):
             x_tile = xin.tile([P, K], BF16, name="x_tile")
             x_tiles.append(x_tile)
 
-        def load_x(i):
-            nc.sync.dma_start(out=x_tiles[i][:], in_=x[i * P : (i + 1) * P, :])
-
-        for i in range(PAIR):
-            load_x(i)
+        for g in range(PASSES):
+            k_cols = slice(g * K_PASS, (g + 1) * K_PASS)
+            nc.sync.dma_start(out=x_tiles[0][:, k_cols], in_=x[0:P, k_cols])
+        nc.sync.dma_start(out=x_tiles[1][:], in_=x[P : 2 * P, :])
         for quadrant in range(4):
             nc.sync.dma_start(
                 out=w_scales[32 * quadrant : 32 * quadrant + 4, :, :].bitcast(I32),
@@ -104,77 +80,77 @@ def tile_modelnew_kernel(tc, x, weight_words, weight_scales, bias, gamma, beta, 
             out=w_codes[:].bitcast(I32),
             in_=weight_words.rearrange("g p n t -> p g (n t)").bitcast(I32),
         )
-        for i in range(PAIR, ROW_TILES):
-            load_x(i)
+        for i in range(2, ROW_TILES):
+            nc.sync.dma_start(out=x_tiles[i][:], in_=x[i * P : (i + 1) * P, :])
 
-        scale_col = const.tile([P, 1], BF16)
-        nc.scalar.dma_start(out=scale_col[:], in_=scale.partition_broadcast(P))
-        nc.scalar.dma_start(out=vec_rows[0:1, 0, :], in_=bias.unsqueeze(0))
-        nc.scalar.dma_start(out=vec_rows[0:1, 1, :], in_=gamma.unsqueeze(0))
-        nc.scalar.dma_start(out=vec_rows[0:1, 2, :], in_=beta.unsqueeze(0))
-
-        bias_ps = psum_acc.tile([P, N], F32, name="acc")
-        nc.tensor.matmul(out=bias_ps[:], lhsT=ones[:], rhs=vec_rows[:, 0, :], start=True, stop=True)
         bias_all = const.tile([P, N], F32)
-        nc.scalar.copy(out=bias_all[:], in_=bias_ps[:])
         gain = psum_const.tile([P, N], F32)
-        nc.tensor.matmul(
-            out=gain[:], lhsT=scale_col[:, 0:1].to_broadcast([P, P]), rhs=vec_rows[:, 1, :], start=True, stop=True
-        )
         shift = psum_const.tile([P, N], F32)
-        nc.tensor.matmul(
-            out=shift[:], lhsT=scale_col[:, 0:1].to_broadcast([P, P]), rhs=vec_rows[:, 2, :], start=True, stop=True
-        )
+        spread = {}
 
-        groups = GROUPS
-        group_of, slot_of = {}, {}
-        for index, members in enumerate(groups):
-            for slot, i in enumerate(members):
-                group_of[i] = index
-                slot_of[i] = slot
+        def spread_vectors(i):
+            bias_ps = psum_acc.tile([P, N], F32, name="acc")
+            nc.tensor.matmul(out=bias_ps[:], lhsT=ones[:], rhs=vec_rows[:, 0, :], start=True, stop=True)
+            spread["bias"] = bias_ps
+            scale_all = scale_col[:, 0:1].to_broadcast([P, P])
+            nc.tensor.matmul(out=gain[:], lhsT=scale_all, rhs=vec_rows[:, 1, :], start=True, stop=True)
+            nc.tensor.matmul(out=shift[:], lhsT=scale_all, rhs=vec_rows[:, 2, :], start=True, stop=True)
 
-        xts, accs, ts, centreds, es, neg_means, row_sums = {}, {}, {}, {}, {}, {}, {}
-        groupeds, codes, zs, sq_sums, rstds, neg_maxs, exp_sums, inv_sums = {}, {}, {}, {}, {}, {}, {}, {}
+        def copy_bias(i):
+            nc.scalar.copy(out=bias_all[:], in_=spread["bias"][:])
+
+        xts, groupeds, codes, accs, ts, centreds, zs, es = {}, {}, {}, {}, {}, {}, {}, {}
+        row_sums, neg_means, sq_sums, rstds, neg_maxs, exp_sums, inv_sums = {}, {}, {}, {}, {}, {}, {}
 
         def transpose_x(i):
             x_words = x_tiles[i][:].bitcast(F32)
-            xt = psum_xt.tile([P, PASSES, HALVES, P], F32, name="xt")
+            xts[i] = []
             for g in range(PASSES):
+                if g == 0 or i == 0:
+                    xt = psum_xt.tile([P, PASSES, HALVES, P], F32, name="xt")
+                xts[i].append(xt)
                 for u in range(HALVES):
                     nc.tensor.transpose(
                         xt[:, g, u, :],
                         x_words[:, (K_PASS // 2) * g + u : (K_PASS // 2) * (g + 1) : HALVES],
                         ident[:],
                     )
-            xts[i] = xt
 
         def regroup_x(i):
-            q, j = group_of[i], slot_of[i]
-            if j == 0:
-                grouped = quant.tile([P, PAIR, PASSES, P, PACK], BF16, align_bytes=64, name="grouped")
-                groupeds[q] = grouped
-            nc.scalar.copy(out=groupeds[q][:, j].bitcast(F32), in_=xts[i][:].rearrange("p g u r -> p g r u"))
+            grouped = quant.tile([P, PASSES, P, PACK], BF16, align_bytes=64, name="grouped")
+            if i == 0:
+                for g in range(PASSES):
+                    nc.scalar.copy(out=grouped[:, g].bitcast(F32), in_=xts[i][g][:, g].rearrange("p u r -> p r u"))
+            else:
+                nc.scalar.copy(out=grouped[:].bitcast(F32), in_=xts[i][0][:].rearrange("p g u r -> p g r u"))
+            groupeds[i] = grouped
 
-        def quantise_x(q):
-            n = len(groups[q])
-            x_codes = quant.tile([P, PAIR, PASSES, P], U32, align_bytes=64, name="x_codes")
-            x_scales = quant.tile([P, PAIR, PASSES, P], U8, align_bytes=64, name="x_scales")
-            nc.vector.quantize_mx(
-                out=x_codes[:, 0:n].rearrange("p j g r -> p (j g r)").bitcast(FP8X4),
-                scales=x_scales[:, 0:n].rearrange("p j g r -> p (j g r)"),
-                in_=groupeds[q][:, 0:n].rearrange("p j g r t -> p (j g r t)"),
-            )
-            codes[q] = (x_codes, x_scales)
+        def quantise_x(i):
+            x_codes = quant.tile([P, PASSES, P], U32, align_bytes=64, name="x_codes")
+            x_scales = quant.tile([P, PASSES, P], U8, align_bytes=64, name="x_scales")
+            if i == 0:
+                for g in range(PASSES):
+                    nc.vector.quantize_mx(
+                        out=x_codes[:, g, :].bitcast(FP8X4),
+                        scales=x_scales[:, g, :],
+                        in_=groupeds[i][:, g].rearrange("p r t -> p (r t)"),
+                    )
+            else:
+                nc.vector.quantize_mx(
+                    out=x_codes[:].rearrange("p g r -> p (g r)").bitcast(FP8X4),
+                    scales=x_scales[:].rearrange("p g r -> p (g r)"),
+                    in_=groupeds[i][:].rearrange("p g r t -> p (g r t)"),
+                )
+            codes[i] = (x_codes, x_scales)
 
         def multiply(i):
-            x_codes, x_scales = codes[group_of[i]]
-            j = slot_of[i]
+            x_codes, x_scales = codes[i]
             acc = psum_acc.tile([P, N], F32, name="acc")
             for g in range(PASSES):
                 nc.tensor.matmul_mx(
                     out=acc[:],
-                    lhsT=x_codes[:, j, g, :].bitcast(FP8X4),
-                    lhsT_scale=x_scales[:, j, g, :],
+                    lhsT=x_codes[:, g, :].bitcast(FP8X4),
+                    lhsT_scale=x_scales[:, g, :],
                     rhs=w_codes[:, g, :].bitcast(FP8X4),
                     rhs_scale=w_scales[:, g, :],
                     start=(g == 0),
@@ -200,25 +176,21 @@ def tile_modelnew_kernel(tc, x, weight_words, weight_scales, bias, gamma, beta, 
             neg_means[i] = neg_mean
 
         def squares_sum(i):
-            q, j = group_of[i], slot_of[i]
-            if j == 0:
-                sq_sum = stats.tile([P, PAIR], F32, name="sq_sum")
-                sq_sums[q] = sq_sum
+            sq_sum = stats.tile([P, 1], F32, name="sq_sum")
             squares = work.tile([P, N], F32, name="squares")
             nc.scalar.activation(
-                out=squares[:], in_=ts[i][:], func=ACT.Square, bias=neg_means[i][:], scale=1.0,
-                accum_out=sq_sums[q][:, j : j + 1],
+                out=squares[:], in_=ts[i][:], func=ACT.Square, bias=neg_means[i][:], scale=1.0, accum_out=sq_sum[:],
             )
+            sq_sums[i] = sq_sum
 
-        def inverse_deviation(q):
-            n = len(groups[q])
-            var_eps = stats.tile([P, PAIR], F32, name="var_eps")
+        def inverse_deviation(i):
+            var_eps = stats.tile([P, 1], F32, name="var_eps")
             nc.gpsimd.tensor_scalar(
-                out=var_eps[:, 0:n], in0=sq_sums[q][:, 0:n], scalar1=1.0 / N, scalar2=EPS, op0=ALU.mult, op1=ALU.add
+                out=var_eps[:], in0=sq_sums[i][:], scalar1=1.0 / N, scalar2=EPS, op0=ALU.mult, op1=ALU.add
             )
-            rstd = stats.tile([P, PAIR], F32, name="rstd")
-            nc.gpsimd.tensor_tensor(out=rstd[:, 0:n], in0=var_eps[:, 0:n], in1=neg_half[:, 0:n], op=ALU.pow)
-            rstds[q] = rstd
+            rstd = stats.tile([P, 1], F32, name="rstd")
+            nc.gpsimd.tensor_tensor(out=rstd[:], in0=var_eps[:], in1=neg_half[:], op=ALU.pow)
+            rstds[i] = rstd
 
         def centre_and_gain(i):
             centred = work.tile([P, N], F32, name="centred")
@@ -228,65 +200,64 @@ def tile_modelnew_kernel(tc, x, weight_words, weight_scales, bias, gamma, beta, 
             centreds[i] = centred
 
         def normalise(i):
-            q, j = group_of[i], slot_of[i]
-            if j == 0:
-                z = pairs.tile([P, PAIR, N], F32, name="z")
-                zs[q] = z
+            z = work.tile([P, N], F32, name="z")
             nc.vector.scalar_tensor_tensor(
-                out=zs[q][:, j, :], in0=centreds[i][:], scalar=rstds[q][:, j : j + 1], in1=shift[:],
-                op0=ALU.mult, op1=ALU.add,
+                out=z[:], in0=centreds[i][:], scalar=rstds[i][:], in1=shift[:], op0=ALU.mult, op1=ALU.add,
             )
+            zs[i] = z
 
-        def row_max(q):
-            n = len(groups[q])
-            neg_max = stats.tile([P, PAIR], F32, name="neg_max")
-            nc.vector.tensor_reduce(out=neg_max[:, 0:n], in_=zs[q][:, 0:n, :], axis=AXIS.X, op=ALU.max, negate=True)
-            neg_maxs[q] = neg_max
+        def row_max(i):
+            neg_max = stats.tile([P, 1], F32, name="neg_max")
+            nc.vector.tensor_reduce(out=neg_max[:], in_=zs[i][:], axis=AXIS.X, op=ALU.max, negate=True)
+            neg_maxs[i] = neg_max
 
         def exponentials(i):
-            q, j = group_of[i], slot_of[i]
-            if j == 0:
-                exp_sum = stats.tile([P, PAIR], F32, name="exp_sum")
-                exp_sums[q] = exp_sum
+            exp_sum = stats.tile([P, 1], F32, name="exp_sum")
             e = work.tile([P, N], F32, name="e")
             nc.scalar.activation(
-                out=e[:], in_=zs[q][:, j, :], func=ACT.Exp, bias=neg_maxs[q][:, j : j + 1], scale=1.0,
-                accum_out=exp_sums[q][:, j : j + 1],
+                out=e[:], in_=zs[i][:], func=ACT.Exp, bias=neg_maxs[i][:], scale=1.0, accum_out=exp_sum[:],
             )
             es[i] = e
+            exp_sums[i] = exp_sum
 
-        def invert_sums(q):
-            n = len(groups[q])
-            inv_sum = stats.tile([P, PAIR], F32, name="inv_sum")
-            if groups[q][0] >= ROW_TILES - TAIL_ON_VECTOR:
-                nc.vector.reciprocal(out=inv_sum[:, 0:n], in_=exp_sums[q][:, 0:n])
+        def invert_sum(i):
+            inv_sum = stats.tile([P, 1], F32, name="inv_sum")
+            if i >= ROW_TILES - TAIL_TILES:
+                nc.vector.reciprocal(out=inv_sum[:], in_=exp_sums[i][:])
             else:
-                nc.gpsimd.tensor_tensor(out=inv_sum[:, 0:n], in0=exp_sums[q][:, 0:n], in1=neg_one[:, 0:n], op=ALU.pow)
-            inv_sums[q] = inv_sum
+                nc.gpsimd.tensor_tensor(out=inv_sum[:], in0=exp_sums[i][:], in1=neg_one[:], op=ALU.pow)
+            inv_sums[i] = inv_sum
 
         def divide_and_store(i):
-            q, j = group_of[i], slot_of[i]
             probs = work.tile([P, N], F32, name="probs")
-            if i >= ROW_TILES - TAIL_ON_VECTOR:
-                nc.vector.tensor_scalar(
-                    out=probs[:], in0=es[i][:], scalar1=inv_sums[q][:, j : j + 1], scalar2=None, op0=ALU.mult
-                )
+            if i >= ROW_TILES - TAIL_TILES:
+                nc.vector.tensor_scalar(out=probs[:], in0=es[i][:], scalar1=inv_sums[i][:], scalar2=None, op0=ALU.mult)
             else:
-                nc.scalar.activation(out=probs[:], in_=es[i][:], func=ACT.Copy, scale=inv_sums[q][:, j : j + 1])
+                nc.scalar.activation(out=probs[:], in_=es[i][:], func=ACT.Copy, scale=inv_sums[i][:])
             nc.sync.dma_start(out=out[i * P : (i + 1) * P, :], in_=probs[:])
 
-        tile_stages = TILE_STAGES(
-            transpose_x, regroup_x, multiply, add_bias, negate_mean, squares_sum, centre_and_gain, normalise,
-            exponentials, divide_and_store,
-        )
-        group_stages = GROUP_STAGES(quantise_x, inverse_deviation, row_max, invert_sums)
-        plan = []
-        for stage, offset, lag, place in tile_stages:
+        stages = [
+            (multiply, -1, 0),
+            (transpose_x, -LEAD, 1),
+            (regroup_x, 1 - LEAD, 2),
+            (invert_sum, 5, 3),
+            (add_bias, 0, 4),
+            (squares_sum, 1, 6),
+            (row_max, 3, 7),
+            (quantise_x, -2, 8),
+            (exponentials, 4, 9),
+            (centre_and_gain, 1, 10),
+            (normalise, 2, 11),
+            (divide_and_store, 5, 12),
+            (negate_mean, 0, 14),
+            (inverse_deviation, 1, 15),
+        ]
+        plan = [(1 - LEAD, 2, -1, spread_vectors), (2 - LEAD, 3, 0, copy_bias)]
+        for stage, offset, place in stages:
             for i in range(ROW_TILES):
-                plan.append((i + offset + lag * (len(groups[group_of[i]]) - 1), place, i, stage))
-        for stage, offset, lag, place in group_stages:
-            for q, members in enumerate(groups):
-                plan.append((members[-1] + offset + lag * (len(members) - 1), place, q, stage))
-        with tc.manual_schedule():
-            for entry in sorted(plan, key=lambda item: item[0:3]):
-                entry[3](entry[2])
+                step = i + offset
+                if stage == transpose_x and i >= HEAD_TILES:
+                    step = max(step, -1)
+                plan.append((step, place, i, stage))
+        for entry in sorted(plan, key=lambda item: item[0:3]):
+            entry[3](entry[2])

@@ -23,6 +23,7 @@ K_PASS = P * PACK
 PASSES = K // K_PASS
 HALVES = 2
 ROW_TILES = M // P
+WARM_UP_MATMULS = 4
 TAIL_TILES = 2
 LEAD = 4
 HEAD_TILES = 2
@@ -60,6 +61,10 @@ def tile_modelnew_kernel(tc, x, weight_words, weight_scales, bias, gamma, beta, 
         make_identity(nc, ident[:])
         table_warm = const.tile([P, 1], F32)
         nc.scalar.activation(out=table_warm[:], in_=neg_half[:], func=ACT.Exp)
+
+        warm = psum_acc.tile([P, P], F32, name="acc")
+        for repeat in range(WARM_UP_MATMULS):
+            nc.tensor.matmul(out=warm[:], lhsT=ident[:], rhs=ident[:], start=True, stop=True)
 
         x_tiles = []
         for i in range(ROW_TILES):

from contextlib import ExitStack

import concourse.mybir as mybir
from concourse.masks import make_identity

F32 = mybir.dt.float32
BF16 = mybir.dt.bfloat16
I32 = mybir.dt.int32
U32 = mybir.dt.uint32
U8 = mybir.dt.uint8
FP8X4 = mybir.dt.float8_e4m3fn_x4
ALU = mybir.AluOpType
ACT = mybir.ActivationFunctionType
AXIS = mybir.AxisListType

M, K, N = 2048, 1024, 512
EPS = 1e-05
FLOPS = 2 * M * K * N

P = 128
PACK = 4
K_PASS = P * PACK
PASSES = K // K_PASS
HALVES = 2
ROW_TILES = M // P
WARM_UP_MATMULS = 4
TAIL_TILES = 2
LEAD = 4
HEAD_TILES = 2


def tile_modelnew_kernel(tc, x, weight_words, weight_scales, bias, gamma, beta, scale, out):
    nc = tc.nc
    with ExitStack() as ctx:
        const = ctx.enter_context(tc.tile_pool(name="const", bufs=1))
        xin = ctx.enter_context(tc.tile_pool(name="xin", bufs=ROW_TILES))
        quant = ctx.enter_context(tc.tile_pool(name="quant", bufs=3))
        work = ctx.enter_context(tc.tile_pool(name="work", bufs=4))
        stats = ctx.enter_context(tc.tile_pool(name="stats", bufs=8))
        psum_const = ctx.enter_context(tc.psum_pool(name="psum_const", bufs=1))
        psum_xt = ctx.enter_context(tc.psum_pool(name="psum_xt", bufs=3))
        psum_acc = ctx.enter_context(tc.psum_pool(name="psum_acc", bufs=3))
        ctx.enter_context(tc.manual_schedule())

        vec_rows = const.tile([P, 3, N], BF16)
        nc.vector.memset(vec_rows[:], 0.0)
        scale_col = const.tile([P, 1], BF16)
        nc.scalar.dma_start(out=scale_col[:], in_=scale.partition_broadcast(P))
        nc.scalar.dma_start(out=vec_rows[0:1, 0, :], in_=bias.unsqueeze(0))
        nc.scalar.dma_start(out=vec_rows[0:1, 1, :], in_=gamma.unsqueeze(0))
        nc.scalar.dma_start(out=vec_rows[0:1, 2, :], in_=beta.unsqueeze(0))
        w_scales = const.tile([P, PASSES, N], U8, align_bytes=64)
        nc.vector.memset(w_scales[:].bitcast(I32), 0)
        ones = const.tile([P, P], BF16)
        nc.vector.memset(ones[:], 1.0)
        neg_half = const.tile([P, 1], F32)
        nc.vector.memset(neg_half[:], -0.5)
        neg_one = const.tile([P, 1], F32)
        nc.vector.memset(neg_one[:], -1.0)
        ident = const.tile([P, P], F32)
        make_identity(nc, ident[:])
        table_warm = const.tile([P, 1], F32)
        nc.scalar.activation(out=table_warm[:], in_=neg_half[:], func=ACT.Exp)

        warm = psum_acc.tile([P, P], F32, name="acc")
        for repeat in range(WARM_UP_MATMULS):
            nc.tensor.matmul(out=warm[:], lhsT=ident[:], rhs=ident[:], start=True, stop=True)

        x_tiles = []
        for i in range(ROW_TILES):
            x_tile = xin.tile([P, K], BF16, name="x_tile")
            x_tiles.append(x_tile)

        for g in range(PASSES):
            k_cols = slice(g * K_PASS, (g + 1) * K_PASS)
            nc.sync.dma_start(out=x_tiles[0][:, k_cols], in_=x[0:P, k_cols])
        nc.sync.dma_start(out=x_tiles[1][:], in_=x[P : 2 * P, :])
        for quadrant in range(4):
            nc.sync.dma_start(
                out=w_scales[32 * quadrant : 32 * quadrant + 4, :, :].bitcast(I32),
                in_=weight_scales[:, 4 * quadrant : 4 * quadrant + 4, :].rearrange("g r n -> r g n").bitcast(I32),
            )
        w_codes = const.tile([P, PASSES, PACK * N], U8, align_bytes=64)
        nc.sync.dma_start(
            out=w_codes[:].bitcast(I32),
            in_=weight_words.rearrange("g p n t -> p g (n t)").bitcast(I32),
        )
        for i in range(2, ROW_TILES):
            nc.sync.dma_start(out=x_tiles[i][:], in_=x[i * P : (i + 1) * P, :])

        bias_all = const.tile([P, N], F32)
        gain = psum_const.tile([P, N], F32)
        shift = psum_const.tile([P, N], F32)
        spread = {}

        def spread_vectors(i):
            bias_ps = psum_acc.tile([P, N], F32, name="acc")
            nc.tensor.matmul(out=bias_ps[:], lhsT=ones[:], rhs=vec_rows[:, 0, :], start=True, stop=True)
            spread["bias"] = bias_ps
            scale_all = scale_col[:, 0:1].to_broadcast([P, P])
            nc.tensor.matmul(out=gain[:], lhsT=scale_all, rhs=vec_rows[:, 1, :], start=True, stop=True)
            nc.tensor.matmul(out=shift[:], lhsT=scale_all, rhs=vec_rows[:, 2, :], start=True, stop=True)

        def copy_bias(i):
            nc.scalar.copy(out=bias_all[:], in_=spread["bias"][:])

        xts, groupeds, codes, accs, ts, centreds, zs, es = {}, {}, {}, {}, {}, {}, {}, {}
        row_sums, neg_means, sq_sums, rstds, neg_maxs, exp_sums, inv_sums = {}, {}, {}, {}, {}, {}, {}

        def transpose_x(i):
            x_words = x_tiles[i][:].bitcast(F32)
            xts[i] = []
            for g in range(PASSES):
                if g == 0 or i == 0:
                    xt = psum_xt.tile([P, PASSES, HALVES, P], F32, name="xt")
                xts[i].append(xt)
                for u in range(HALVES):
                    nc.tensor.transpose(
                        xt[:, g, u, :],
                        x_words[:, (K_PASS // 2) * g + u : (K_PASS // 2) * (g + 1) : HALVES],
                        ident[:],
                    )

        def regroup_x(i):
            grouped = quant.tile([P, PASSES, P, PACK], BF16, align_bytes=64, name="grouped")
            if i == 0:
                for g in range(PASSES):
                    nc.scalar.copy(out=grouped[:, g].bitcast(F32), in_=xts[i][g][:, g].rearrange("p u r -> p r u"))
            else:
                nc.scalar.copy(out=grouped[:].bitcast(F32), in_=xts[i][0][:].rearrange("p g u r -> p g r u"))
            groupeds[i] = grouped

        def quantise_x(i):
            x_codes = quant.tile([P, PASSES, P], U32, align_bytes=64, name="x_codes")
            x_scales = quant.tile([P, PASSES, P], U8, align_bytes=64, name="x_scales")
            if i == 0:
                for g in range(PASSES):
                    nc.vector.quantize_mx(
                        out=x_codes[:, g, :].bitcast(FP8X4),
                        scales=x_scales[:, g, :],
                        in_=groupeds[i][:, g].rearrange("p r t -> p (r t)"),
                    )
            else:
                nc.vector.quantize_mx(
                    out=x_codes[:].rearrange("p g r -> p (g r)").bitcast(FP8X4),
                    scales=x_scales[:].rearrange("p g r -> p (g r)"),
                    in_=groupeds[i][:].rearrange("p g r t -> p (g r t)"),
                )
            codes[i] = (x_codes, x_scales)

        def multiply(i):
            x_codes, x_scales = codes[i]
            acc = psum_acc.tile([P, N], F32, name="acc")
            for g in range(PASSES):
                nc.tensor.matmul_mx(
                    out=acc[:],
                    lhsT=x_codes[:, g, :].bitcast(FP8X4),
                    lhsT_scale=x_scales[:, g, :],
                    rhs=w_codes[:, g, :].bitcast(FP8X4),
                    rhs_scale=w_scales[:, g, :],
                    start=(g == 0),
                    stop=(g == PASSES - 1),
                )
            accs[i] = acc

        def add_bias(i):
            row_sum = stats.tile([P, 1], F32, name="row_sum")
            t = work.tile([P, N], F32, name="t")
            nc.vector.scalar_tensor_tensor(
                out=t[:], in0=accs[i][:], scalar=1.0, in1=bias_all[:], op0=ALU.mult, op1=ALU.add,
                accum_out=row_sum[:],
            )
            ts[i] = t
            row_sums[i] = row_sum

        def negate_mean(i):
            neg_mean = stats.tile([P, 1], F32, name="neg_mean")
            nc.gpsimd.tensor_scalar(
                out=neg_mean[:], in0=row_sums[i][:], scalar1=-1.0 / N, scalar2=0.0, op0=ALU.mult, op1=ALU.add
            )
            neg_means[i] = neg_mean

        def squares_sum(i):
            sq_sum = stats.tile([P, 1], F32, name="sq_sum")
            squares = work.tile([P, N], F32, name="squares")
            nc.scalar.activation(
                out=squares[:], in_=ts[i][:], func=ACT.Square, bias=neg_means[i][:], scale=1.0, accum_out=sq_sum[:],
            )
            sq_sums[i] = sq_sum

        def inverse_deviation(i):
            var_eps = stats.tile([P, 1], F32, name="var_eps")
            nc.gpsimd.tensor_scalar(
                out=var_eps[:], in0=sq_sums[i][:], scalar1=1.0 / N, scalar2=EPS, op0=ALU.mult, op1=ALU.add
            )
            rstd = stats.tile([P, 1], F32, name="rstd")
            nc.gpsimd.tensor_tensor(out=rstd[:], in0=var_eps[:], in1=neg_half[:], op=ALU.pow)
            rstds[i] = rstd

        def centre_and_gain(i):
            centred = work.tile([P, N], F32, name="centred")
            nc.vector.scalar_tensor_tensor(
                out=centred[:], in0=ts[i][:], scalar=neg_means[i][:], in1=gain[:], op0=ALU.add, op1=ALU.mult,
            )
            centreds[i] = centred

        def normalise(i):
            z = work.tile([P, N], F32, name="z")
            nc.vector.scalar_tensor_tensor(
                out=z[:], in0=centreds[i][:], scalar=rstds[i][:], in1=shift[:], op0=ALU.mult, op1=ALU.add,
            )
            zs[i] = z

        def row_max(i):
            neg_max = stats.tile([P, 1], F32, name="neg_max")
            nc.vector.tensor_reduce(out=neg_max[:], in_=zs[i][:], axis=AXIS.X, op=ALU.max, negate=True)
            neg_maxs[i] = neg_max

        def exponentials(i):
            exp_sum = stats.tile([P, 1], F32, name="exp_sum")
            e = work.tile([P, N], F32, name="e")
            nc.scalar.activation(
                out=e[:], in_=zs[i][:], func=ACT.Exp, bias=neg_maxs[i][:], scale=1.0, accum_out=exp_sum[:],
            )
            es[i] = e
            exp_sums[i] = exp_sum

        def invert_sum(i):
            inv_sum = stats.tile([P, 1], F32, name="inv_sum")
            if i >= ROW_TILES - TAIL_TILES:
                nc.vector.reciprocal(out=inv_sum[:], in_=exp_sums[i][:])
            else:
                nc.gpsimd.tensor_tensor(out=inv_sum[:], in0=exp_sums[i][:], in1=neg_one[:], op=ALU.pow)
            inv_sums[i] = inv_sum

        def divide_and_store(i):
            probs = work.tile([P, N], F32, name="probs")
            if i >= ROW_TILES - TAIL_TILES:
                nc.vector.tensor_scalar(out=probs[:], in0=es[i][:], scalar1=inv_sums[i][:], scalar2=None, op0=ALU.mult)
            else:
                nc.scalar.activation(out=probs[:], in_=es[i][:], func=ACT.Copy, scale=inv_sums[i][:])
            nc.sync.dma_start(out=out[i * P : (i + 1) * P, :], in_=probs[:])

        stages = [
            (multiply, -1, 0),
            (transpose_x, -LEAD, 1),
            (regroup_x, 1 - LEAD, 2),
            (invert_sum, 5, 3),
            (add_bias, 0, 4),
            (squares_sum, 1, 6),
            (row_max, 3, 7),
            (quantise_x, -2, 8),
            (exponentials, 4, 9),
            (centre_and_gain, 1, 10),
            (normalise, 2, 11),
            (divide_and_store, 5, 12),
            (negate_mean, 0, 14),
            (inverse_deviation, 1, 15),
        ]
        plan = [(1 - LEAD, 2, -1, spread_vectors), (2 - LEAD, 3, 0, copy_bias)]
        for stage, offset, place in stages:
            for i in range(ROW_TILES):
                step = i + offset
                if stage == transpose_x and i >= HEAD_TILES:
                    step = max(step, -1)
                plan.append((step, place, i, stage))
        for entry in sorted(plan, key=lambda item: item[0:3]):
            entry[3](entry[2])
